import numpy as np
import ml_dtypes

BF16 = ml_dtypes.bfloat16


def bf(x):
    return np.asarray(x, np.float32).astype(BF16)


def f32(x):
    return np.asarray(x, np.float32)


def f64(x):
    return np.asarray(x).astype(np.float64)


def striped(idx):
    return np.tile(idx.reshape(-1, 16).T, (8, 1))


F, S, A, M, N, H, K = 128, 256, 8, 256, 2048, 128, 16


def setup_inputs():
    bound = np.sqrt(2.0) * np.sqrt(6.0 / (F + F + M))
    return {
        "table": bf(np.random.standard_normal((F, S))),
        "w_nb": bf(np.random.uniform(-bound, bound, (F, M))),
        "w_self": bf(np.random.uniform(-bound, bound, (F, M))),
        "b": f32(0.1 * np.random.standard_normal((M, 1))),
        "dist": f32(0.5 + np.random.uniform(size=(1, N))),
        "score": f32(0.5 + np.random.uniform(size=(1, A))),
        "offs": striped(np.concatenate([np.random.permutation(S)[:H] for _ in range(K)])),
    }


def reference(table, w_nb, w_self, b, dist, score, offs):
    idx = offs[:16].T.reshape(-1)
    t = f64(table)
    d = (f64(dist).reshape(S, A) * f64(score)).reshape(1, N)
    nb = f64(w_nb).T @ t[:, idx]
    own = f64(w_self).T @ t + f64(b)
    h = np.maximum(nb * d + np.repeat(own, A, axis=1), 0.0)
    return h.reshape(M, S, A).mean(axis=2)

@@ -1,0 +1,89 @@
+import concourse.mybir as mybir
+
+BF16, F32, U16 = mybir.dt.bfloat16, mybir.dt.float32, mybir.dt.uint16
+MULT, ADD = mybir.AluOpType.mult, mybir.AluOpType.add
+IDENTITY = mybir.ActivationFunctionType.Identity
+RELU = mybir.ActivationFunctionType.Relu
+
+P = 128
+NODES = 256
+ANCHORS = 8
+ENTRIES = NODES * ANCHORS
+BLOCKS = 2
+PIECE = NODES
+PIECE_COLS = PIECE // 16
+CHUNK = 512
+CHUNKS = ENTRIES // CHUNK
+CHUNK_NODES = CHUNK // ANCHORS
+
+FLOPS = 2 * P * (BLOCKS * P) * (ENTRIES + NODES)
+
+
+def tile_p_a_gin_kernel(tc, table, w_nb, w_self, b, dist, score, offs, out):
+    nc = tc.nc
+    with (
+        tc.tile_pool(name="held", bufs=1) as held,
+        tc.tile_pool(name="work", bufs=3) as work,
+        tc.psum_pool(name="psum", bufs=8) as psum,
+    ):
+        offsets = held.tile([P, ENTRIES // 16], U16, name="offsets")
+        nc.sync.dma_start(offsets[:], offs)
+        table_sb = held.tile([P, NODES], BF16, name="table_sb")
+        nc.sync.dma_start(table_sb[:], table)
+        w_nb_sb = held.tile([P, BLOCKS * P], BF16, name="w_nb_sb")
+        nc.sync.dma_start(w_nb_sb[:], w_nb)
+        w_self_sb = held.tile([P, BLOCKS * P], BF16, name="w_self_sb")
+        nc.scalar.dma_start(w_self_sb[:], w_self)
+        score_sb = held.tile([P, ANCHORS], F32, name="score_sb")
+        nc.scalar.dma_start(score_sb[:], score.broadcast_to([P, ANCHORS]))
+        dist_sb = [held.tile([P, CHUNK], F32, name=f"dist_sb{c}") for c in range(CHUNKS)]
+        for c in range(CHUNKS):
+            queue = nc.scalar if c % 2 == 0 else nc.sync
+            queue.dma_start(dist_sb[c][:], dist[:, c * CHUNK : (c + 1) * CHUNK].broadcast_to([P, CHUNK]))
+        b_sb = [held.tile([P, 1], F32, name=f"b_sb{k}") for k in range(BLOCKS)]
+        for k in range(BLOCKS):
+            nc.gpsimd.dma_start(b_sb[k][:], b[k * P : (k + 1) * P, :])
+
+        own = [held.tile([P, NODES], F32, name=f"own{k}") for k in range(BLOCKS)]
+        for k in range(BLOCKS):
+            own_ps = psum.tile([P, CHUNK], F32, name="bank")
+            nc.tensor.matmul(own_ps[:, :NODES], w_self_sb[:, k * P : (k + 1) * P], table_sb[:], start=True, stop=True)
+            nc.scalar.activation(own[k][:], own_ps[:, :NODES], IDENTITY, bias=b_sb[k][:], scale=1.0)
+
+        mean = [held.tile([P, NODES], F32, name=f"mean{k}") for k in range(BLOCKS)]
+        for c in range(CHUNKS):
+            nodes = slice(c * CHUNK_NODES, (c + 1) * CHUNK_NODES)
+            d = work.tile([P, CHUNK_NODES, ANCHORS], F32, name="d")
+            nc.vector.tensor_tensor(
+                d[:],
+                dist_sb[c][:].rearrange("p (n a) -> p n a", a=ANCHORS),
+                score_sb[:].unsqueeze(1).to_broadcast([P, CHUNK_NODES, ANCHORS]),
+                MULT,
+            )
+            for k in range(BLOCKS):
+                bank = psum.tile([P, CHUNK], F32, name="bank")
+                for half in range(CHUNK // PIECE):
+                    piece = c * (CHUNK // PIECE) + half
+                    nc.tensor.matmul(
+                        bank[:, half * PIECE : (half + 1) * PIECE],
+                        w_nb_sb[:, k * P : (k + 1) * P],
+                        table_sb[:].indirect(offsets[:, piece * PIECE_COLS : (piece + 1) * PIECE_COLS]),
+                        start=True,
+                        stop=True,
+                    )
+                scaled = work.tile([P, CHUNK_NODES, ANCHORS], F32, name="scaled")
+                nc.vector.tensor_tensor(scaled[:], bank[:].rearrange("p (n a) -> p n a", a=ANCHORS), d[:], MULT)
+                summed = work.tile([P, CHUNK_NODES, ANCHORS], F32, name="summed")
+                nc.vector.tensor_tensor(
+                    summed[:],
+                    scaled[:],
+                    own[k][:, nodes].unsqueeze(2).to_broadcast([P, CHUNK_NODES, ANCHORS]),
+                    ADD,
+                )
+                hidden = work.tile([P, CHUNK_NODES, ANCHORS], F32, name="hidden")
+                nc.scalar.activation(hidden[:], summed[:], RELU, scale=1.0 / ANCHORS)
+                nc.vector.tensor_reduce(mean[k][:, nodes], hidden[:], axis=mybir.AxisListType.X, op=ADD)
+
+        for k in range(BLOCKS):
+            queue = nc.sync if k == 0 else nc.scalar
+            queue.dma_start(out[k * P : (k + 1) * P, :], mean[k][:])

@@ -23,7 +23,7 @@ def tile_p_a_gin_kernel(tc, table, w_nb, w_self, b, dist, score, offs, out):
     nc = tc.nc
     with (
         tc.tile_pool(name="held", bufs=1) as held,
-        tc.tile_pool(name="work", bufs=3) as work,
+        tc.tile_pool(name="work", bufs=4) as work,
         tc.psum_pool(name="psum", bufs=8) as psum,
     ):
         offsets = held.tile([P, ENTRIES // 16], U16, name="offsets")
@@ -34,15 +34,15 @@ def tile_p_a_gin_kernel(tc, table, w_nb, w_self, b, dist, score, offs, out):
         nc.sync.dma_start(w_nb_sb[:], w_nb)
         w_self_sb = held.tile([P, BLOCKS * P], BF16, name="w_self_sb")
         nc.scalar.dma_start(w_self_sb[:], w_self)
+        b_sb = [held.tile([P, 1], F32, name=f"b_sb{k}") for k in range(BLOCKS)]
+        for k in range(BLOCKS):
+            nc.sync.dma_start(b_sb[k][:], b[k * P : (k + 1) * P, :])
         score_sb = held.tile([P, ANCHORS], F32, name="score_sb")
         nc.scalar.dma_start(score_sb[:], score.broadcast_to([P, ANCHORS]))
         dist_sb = [held.tile([P, CHUNK], F32, name=f"dist_sb{c}") for c in range(CHUNKS)]
         for c in range(CHUNKS):
             queue = nc.scalar if c % 2 == 0 else nc.sync
             queue.dma_start(dist_sb[c][:], dist[:, c * CHUNK : (c + 1) * CHUNK].broadcast_to([P, CHUNK]))
-        b_sb = [held.tile([P, 1], F32, name=f"b_sb{k}") for k in range(BLOCKS)]
-        for k in range(BLOCKS):
-            nc.gpsimd.dma_start(b_sb[k][:], b[k * P : (k + 1) * P, :])
 
         own = [held.tile([P, NODES], F32, name=f"own{k}") for k in range(BLOCKS)]
         for k in range(BLOCKS):
@@ -74,7 +74,7 @@ def tile_p_a_gin_kernel(tc, table, w_nb, w_self, b, dist, score, offs, out):
                 scaled = work.tile([P, CHUNK_NODES, ANCHORS], F32, name="scaled")
                 nc.vector.tensor_tensor(scaled[:], bank[:].rearrange("p (n a) -> p n a", a=ANCHORS), d[:], MULT)
                 summed = work.tile([P, CHUNK_NODES, ANCHORS], F32, name="summed")
-                nc.vector.tensor_tensor(
+                nc.gpsimd.tensor_tensor(
                     summed[:],
                     scaled[:],
                     own[k][:, nodes].unsqueeze(2).to_broadcast([P, CHUNK_NODES, ANCHORS]),

@@ -2,7 +2,6 @@ import concourse.mybir as mybir
 
 BF16, F32, U16 = mybir.dt.bfloat16, mybir.dt.float32, mybir.dt.uint16
 MULT, ADD = mybir.AluOpType.mult, mybir.AluOpType.add
-IDENTITY = mybir.ActivationFunctionType.Identity
 RELU = mybir.ActivationFunctionType.Relu
 
 P = 128
@@ -15,6 +14,7 @@ PIECE_COLS = PIECE // 16
 CHUNK = 512
 CHUNKS = ENTRIES // CHUNK
 CHUNK_NODES = CHUNK // ANCHORS
+VECTOR_ADDS_FROM = CHUNKS - 1
 
 FLOPS = 2 * P * (BLOCKS * P) * (ENTRIES + NODES)
 
@@ -24,7 +24,8 @@ def tile_p_a_gin_kernel(tc, table, w_nb, w_self, b, dist, score, offs, out):
     with (
         tc.tile_pool(name="held", bufs=1) as held,
         tc.tile_pool(name="work", bufs=4) as work,
-        tc.psum_pool(name="psum", bufs=8) as psum,
+        tc.psum_pool(name="kept", bufs=1) as kept,
+        tc.psum_pool(name="psum", bufs=5) as psum,
     ):
         offsets = held.tile([P, ENTRIES // 16], U16, name="offsets")
         nc.sync.dma_start(offsets[:], offs)
@@ -34,30 +35,39 @@ def tile_p_a_gin_kernel(tc, table, w_nb, w_self, b, dist, score, offs, out):
         nc.sync.dma_start(w_nb_sb[:], w_nb)
         w_self_sb = held.tile([P, BLOCKS * P], BF16, name="w_self_sb")
         nc.scalar.dma_start(w_self_sb[:], w_self)
-        b_sb = [held.tile([P, 1], F32, name=f"b_sb{k}") for k in range(BLOCKS)]
-        for k in range(BLOCKS):
-            nc.sync.dma_start(b_sb[k][:], b[k * P : (k + 1) * P, :])
-        score_sb = held.tile([P, ANCHORS], F32, name="score_sb")
-        nc.scalar.dma_start(score_sb[:], score.broadcast_to([P, ANCHORS]))
+        score_row = held.tile([1, ANCHORS], F32, name="score_row")
+        nc.scalar.dma_start(score_row[:], score)
         dist_sb = [held.tile([P, CHUNK], F32, name=f"dist_sb{c}") for c in range(CHUNKS)]
         for c in range(CHUNKS):
             queue = nc.scalar if c % 2 == 0 else nc.sync
             queue.dma_start(dist_sb[c][:], dist[:, c * CHUNK : (c + 1) * CHUNK].broadcast_to([P, CHUNK]))
-
-        own = [held.tile([P, NODES], F32, name=f"own{k}") for k in range(BLOCKS)]
+        b_sb = [held.tile([P, 1], F32, name=f"b_sb{k}") for k in range(BLOCKS)]
         for k in range(BLOCKS):
-            own_ps = psum.tile([P, CHUNK], F32, name="bank")
-            nc.tensor.matmul(own_ps[:, :NODES], w_self_sb[:, k * P : (k + 1) * P], table_sb[:], start=True, stop=True)
-            nc.scalar.activation(own[k][:], own_ps[:, :NODES], IDENTITY, bias=b_sb[k][:], scale=1.0)
+            nc.sync.dma_start(b_sb[k][:], b[k * P : (k + 1) * P, :])
 
-        mean = [held.tile([P, NODES], F32, name=f"mean{k}") for k in range(BLOCKS)]
+        own_ps = [kept.tile([P, NODES], F32, name=f"own_ps{k}") for k in range(BLOCKS)]
+        own_sb = [held.tile([P, NODES], F32, name=f"own_sb{k}") for k in range(BLOCKS)]
+        for k in range(BLOCKS):
+            nc.tensor.matmul(own_ps[k][:], w_self_sb[:, k * P : (k + 1) * P], table_sb[:], start=True, stop=True)
+            nc.scalar.copy(own_sb[k][:], own_ps[k][:])
+        b_mean = [held.tile([P, 1], F32, name=f"b_mean{k}") for k in range(BLOCKS)]
+        for k in range(BLOCKS):
+            nc.scalar.mul(b_mean[k][:], b_sb[k][:], 1.0 / ANCHORS)
+
+        ones_row = held.tile([1, P], F32, name="ones_row")
+        nc.vector.memset(ones_row[:], 1.0)
+        score_ps = kept.tile([P, ANCHORS], F32, name="score_ps")
+        nc.tensor.matmul(score_ps[:], ones_row[:], score_row[:], start=True, stop=True)
+
+        banks = [(c, k) for c in range(CHUNKS) for k in range(BLOCKS)]
+
+        scaled = {}
         for c in range(CHUNKS):
-            nodes = slice(c * CHUNK_NODES, (c + 1) * CHUNK_NODES)
             d = work.tile([P, CHUNK_NODES, ANCHORS], F32, name="d")
             nc.vector.tensor_tensor(
                 d[:],
                 dist_sb[c][:].rearrange("p (n a) -> p n a", a=ANCHORS),
-                score_sb[:].unsqueeze(1).to_broadcast([P, CHUNK_NODES, ANCHORS]),
+                score_ps[:].unsqueeze(1).to_broadcast([P, CHUNK_NODES, ANCHORS]),
                 MULT,
             )
             for k in range(BLOCKS):
@@ -71,18 +81,27 @@ def tile_p_a_gin_kernel(tc, table, w_nb, w_self, b, dist, score, offs, out):
                         start=True,
                         stop=True,
                     )
-                scaled = work.tile([P, CHUNK_NODES, ANCHORS], F32, name="scaled")
-                nc.vector.tensor_tensor(scaled[:], bank[:].rearrange("p (n a) -> p n a", a=ANCHORS), d[:], MULT)
-                summed = work.tile([P, CHUNK_NODES, ANCHORS], F32, name="summed")
-                nc.gpsimd.tensor_tensor(
-                    summed[:],
-                    scaled[:],
-                    own[k][:, nodes].unsqueeze(2).to_broadcast([P, CHUNK_NODES, ANCHORS]),
-                    ADD,
-                )
-                hidden = work.tile([P, CHUNK_NODES, ANCHORS], F32, name="hidden")
-                nc.scalar.activation(hidden[:], summed[:], RELU, scale=1.0 / ANCHORS)
-                nc.vector.tensor_reduce(mean[k][:, nodes], hidden[:], axis=mybir.AxisListType.X, op=ADD)
+                scaled[c, k] = held.tile([P, CHUNK_NODES, ANCHORS], F32, name=f"scaled{c}_{k}")
+                nc.vector.tensor_tensor(scaled[c, k][:], bank[:].rearrange("p (n a) -> p n a", a=ANCHORS), d[:], MULT)
+
+        summed = {}
+        for c, k in banks:
+            nodes = slice(c * CHUNK_NODES, (c + 1) * CHUNK_NODES)
+            summed[c, k] = held.tile([P, CHUNK_NODES, ANCHORS], F32, name=f"summed{c}_{k}")
+            engine, own = (nc.gpsimd, own_sb[k]) if c < VECTOR_ADDS_FROM else (nc.vector, own_ps[k])
+            engine.tensor_tensor(
+                summed[c, k][:],
+                scaled[c, k][:],
+                own[:, nodes].unsqueeze(2).to_broadcast([P, CHUNK_NODES, ANCHORS]),
+                ADD,
+            )
+
+        mean = [held.tile([P, NODES], F32, name=f"mean{k}") for k in range(BLOCKS)]
+        for c, k in banks:
+            nodes = slice(c * CHUNK_NODES, (c + 1) * CHUNK_NODES)
+            hidden = work.tile([P, CHUNK_NODES, ANCHORS], F32, name="hidden")
+            nc.scalar.activation(hidden[:], summed[c, k][:], RELU, bias=b_mean[k][:], scale=1.0 / ANCHORS)
+            nc.vector.tensor_reduce(mean[k][:, nodes], hidden[:], axis=mybir.AxisListType.X, op=ADD)
 
         for k in range(BLOCKS):
             queue = nc.sync if k == 0 else nc.scalar

@@ -2,7 +2,7 @@ import concourse.mybir as mybir
 
 BF16, F32, U16 = mybir.dt.bfloat16, mybir.dt.float32, mybir.dt.uint16
 MULT, ADD = mybir.AluOpType.mult, mybir.AluOpType.add
-RELU = mybir.ActivationFunctionType.Relu
+RELU, COPY = mybir.ActivationFunctionType.Relu, mybir.ActivationFunctionType.Copy
 
 P = 128
 NODES = 256
@@ -14,7 +14,7 @@ PIECE_COLS = PIECE // 16
 CHUNK = 512
 CHUNKS = ENTRIES // CHUNK
 CHUNK_NODES = CHUNK // ANCHORS
-VECTOR_ADDS_FROM = CHUNKS - 1
+VECTOR_CHUNK = CHUNKS - 2
 
 FLOPS = 2 * P * (BLOCKS * P) * (ENTRIES + NODES)
 
@@ -25,7 +25,7 @@ def tile_p_a_gin_kernel(tc, table, w_nb, w_self, b, dist, score, offs, out):
         tc.tile_pool(name="held", bufs=1) as held,
         tc.tile_pool(name="work", bufs=4) as work,
         tc.psum_pool(name="kept", bufs=1) as kept,
-        tc.psum_pool(name="psum", bufs=5) as psum,
+        tc.psum_pool(name="psum", bufs=6) as psum,
     ):
         offsets = held.tile([P, ENTRIES // 16], U16, name="offsets")
         nc.sync.dma_start(offsets[:], offs)
@@ -35,8 +35,8 @@ def tile_p_a_gin_kernel(tc, table, w_nb, w_self, b, dist, score, offs, out):
         nc.sync.dma_start(w_nb_sb[:], w_nb)
         w_self_sb = held.tile([P, BLOCKS * P], BF16, name="w_self_sb")
         nc.scalar.dma_start(w_self_sb[:], w_self)
-        score_row = held.tile([1, ANCHORS], F32, name="score_row")
-        nc.scalar.dma_start(score_row[:], score)
+        score_sb = held.tile([P, ANCHORS], F32, name="score_sb")
+        nc.scalar.dma_start(score_sb[:], score.broadcast_to([P, ANCHORS]))
         dist_sb = [held.tile([P, CHUNK], F32, name=f"dist_sb{c}") for c in range(CHUNKS)]
         for c in range(CHUNKS):
             queue = nc.scalar if c % 2 == 0 else nc.sync
@@ -50,26 +50,14 @@ def tile_p_a_gin_kernel(tc, table, w_nb, w_self, b, dist, score, offs, out):
         for k in range(BLOCKS):
             nc.tensor.matmul(own_ps[k][:], w_self_sb[:, k * P : (k + 1) * P], table_sb[:], start=True, stop=True)
             nc.scalar.copy(own_sb[k][:], own_ps[k][:])
-        b_mean = [held.tile([P, 1], F32, name=f"b_mean{k}") for k in range(BLOCKS)]
-        for k in range(BLOCKS):
-            nc.scalar.mul(b_mean[k][:], b_sb[k][:], 1.0 / ANCHORS)
-
-        ones_row = held.tile([1, P], F32, name="ones_row")
-        nc.vector.memset(ones_row[:], 1.0)
-        score_ps = kept.tile([P, ANCHORS], F32, name="score_ps")
-        nc.tensor.matmul(score_ps[:], ones_row[:], score_row[:], start=True, stop=True)
-
         banks = [(c, k) for c in range(CHUNKS) for k in range(BLOCKS)]
 
         scaled = {}
         for c in range(CHUNKS):
-            d = work.tile([P, CHUNK_NODES, ANCHORS], F32, name="d")
-            nc.vector.tensor_tensor(
-                d[:],
-                dist_sb[c][:].rearrange("p (n a) -> p n a", a=ANCHORS),
-                score_ps[:].unsqueeze(1).to_broadcast([P, CHUNK_NODES, ANCHORS]),
-                MULT,
-            )
+            d = work.tile([P, ANCHORS, CHUNK_NODES], F32, name="d")
+            dist_by_anchor = dist_sb[c][:].rearrange("p (n a) -> p a n", a=ANCHORS)
+            for a in range(ANCHORS):
+                nc.scalar.activation(d[:, a : a + 1, :], dist_by_anchor[:, a : a + 1, :], COPY, scale=score_sb[:, a : a + 1])
             for k in range(BLOCKS):
                 bank = psum.tile([P, CHUNK], F32, name="bank")
                 for half in range(CHUNK // PIECE):
@@ -82,13 +70,18 @@ def tile_p_a_gin_kernel(tc, table, w_nb, w_self, b, dist, score, offs, out):
                         stop=True,
                     )
                 scaled[c, k] = held.tile([P, CHUNK_NODES, ANCHORS], F32, name=f"scaled{c}_{k}")
-                nc.vector.tensor_tensor(scaled[c, k][:], bank[:].rearrange("p (n a) -> p n a", a=ANCHORS), d[:], MULT)
+                nc.vector.tensor_tensor(
+                    scaled[c, k][:],
+                    bank[:].rearrange("p (n a) -> p n a", a=ANCHORS),
+                    d[:].rearrange("p a n -> p n a"),
+                    MULT,
+                )
 
         summed = {}
         for c, k in banks:
             nodes = slice(c * CHUNK_NODES, (c + 1) * CHUNK_NODES)
             summed[c, k] = held.tile([P, CHUNK_NODES, ANCHORS], F32, name=f"summed{c}_{k}")
-            engine, own = (nc.gpsimd, own_sb[k]) if c < VECTOR_ADDS_FROM else (nc.vector, own_ps[k])
+            engine, own = (nc.vector, own_ps[k]) if c == VECTOR_CHUNK else (nc.gpsimd, own_sb[k])
             engine.tensor_tensor(
                 summed[c, k][:],
                 scaled[c, k][:],
@@ -96,6 +89,9 @@ def tile_p_a_gin_kernel(tc, table, w_nb, w_self, b, dist, score, offs, out):
                 ADD,
             )
 
+        b_mean = [held.tile([P, 1], F32, name=f"b_mean{k}") for k in range(BLOCKS)]
+        for k in range(BLOCKS):
+            nc.scalar.mul(b_mean[k][:], b_sb[k][:], 1.0 / ANCHORS)
         mean = [held.tile([P, NODES], F32, name=f"mean{k}") for k in range(BLOCKS)]
         for c, k in banks:
             nodes = slice(c * CHUNK_NODES, (c + 1) * CHUNK_NODES)

@@ -2,7 +2,7 @@ import concourse.mybir as mybir
 
 BF16, F32, U16 = mybir.dt.bfloat16, mybir.dt.float32, mybir.dt.uint16
 MULT, ADD = mybir.AluOpType.mult, mybir.AluOpType.add
-RELU, COPY = mybir.ActivationFunctionType.Relu, mybir.ActivationFunctionType.Copy
+RELU = mybir.ActivationFunctionType.Relu
 
 P = 128
 NODES = 256
@@ -25,7 +25,7 @@ def tile_p_a_gin_kernel(tc, table, w_nb, w_self, b, dist, score, offs, out):
         tc.tile_pool(name="held", bufs=1) as held,
         tc.tile_pool(name="work", bufs=4) as work,
         tc.psum_pool(name="kept", bufs=1) as kept,
-        tc.psum_pool(name="psum", bufs=6) as psum,
+        tc.psum_pool(name="psum", bufs=5) as psum,
     ):
         offsets = held.tile([P, ENTRIES // 16], U16, name="offsets")
         nc.sync.dma_start(offsets[:], offs)
@@ -50,14 +50,18 @@ def tile_p_a_gin_kernel(tc, table, w_nb, w_self, b, dist, score, offs, out):
         for k in range(BLOCKS):
             nc.tensor.matmul(own_ps[k][:], w_self_sb[:, k * P : (k + 1) * P], table_sb[:], start=True, stop=True)
             nc.scalar.copy(own_sb[k][:], own_ps[k][:])
+
         banks = [(c, k) for c in range(CHUNKS) for k in range(BLOCKS)]
 
         scaled = {}
         for c in range(CHUNKS):
-            d = work.tile([P, ANCHORS, CHUNK_NODES], F32, name="d")
-            dist_by_anchor = dist_sb[c][:].rearrange("p (n a) -> p a n", a=ANCHORS)
-            for a in range(ANCHORS):
-                nc.scalar.activation(d[:, a : a + 1, :], dist_by_anchor[:, a : a + 1, :], COPY, scale=score_sb[:, a : a + 1])
+            d = work.tile([P, CHUNK_NODES, ANCHORS], F32, name="d")
+            nc.vector.tensor_tensor(
+                d[:],
+                dist_sb[c][:].rearrange("p (n a) -> p n a", a=ANCHORS),
+                score_sb[:].unsqueeze(1).to_broadcast([P, CHUNK_NODES, ANCHORS]),
+                MULT,
+            )
             for k in range(BLOCKS):
                 bank = psum.tile([P, CHUNK], F32, name="bank")
                 for half in range(CHUNK // PIECE):
@@ -70,22 +74,17 @@ def tile_p_a_gin_kernel(tc, table, w_nb, w_self, b, dist, score, offs, out):
                         stop=True,
                     )
                 scaled[c, k] = held.tile([P, CHUNK_NODES, ANCHORS], F32, name=f"scaled{c}_{k}")
-                nc.vector.tensor_tensor(
-                    scaled[c, k][:],
-                    bank[:].rearrange("p (n a) -> p n a", a=ANCHORS),
-                    d[:].rearrange("p a n -> p n a"),
-                    MULT,
-                )
+                nc.vector.tensor_tensor(scaled[c, k][:], bank[:].rearrange("p (n a) -> p n a", a=ANCHORS), d[:], MULT)
 
         summed = {}
         for c, k in banks:
             nodes = slice(c * CHUNK_NODES, (c + 1) * CHUNK_NODES)
             summed[c, k] = held.tile([P, CHUNK_NODES, ANCHORS], F32, name=f"summed{c}_{k}")
-            engine, own = (nc.vector, own_ps[k]) if c == VECTOR_CHUNK else (nc.gpsimd, own_sb[k])
+            engine = nc.vector if c == VECTOR_CHUNK else nc.gpsimd
             engine.tensor_tensor(
                 summed[c, k][:],
                 scaled[c, k][:],
-                own[:, nodes].unsqueeze(2).to_broadcast([P, CHUNK_NODES, ANCHORS]),
+                own_sb[k][:, nodes].unsqueeze(2).to_broadcast([P, CHUNK_NODES, ANCHORS]),
                 ADD,
             )
 

@@ -25,7 +25,7 @@ def tile_p_a_gin_kernel(tc, table, w_nb, w_self, b, dist, score, offs, out):
         tc.tile_pool(name="held", bufs=1) as held,
         tc.tile_pool(name="work", bufs=4) as work,
         tc.psum_pool(name="kept", bufs=1) as kept,
-        tc.psum_pool(name="psum", bufs=5) as psum,
+        tc.psum_pool(name="psum", bufs=6) as psum,
     ):
         offsets = held.tile([P, ENTRIES // 16], U16, name="offsets")
         nc.sync.dma_start(offsets[:], offs)
@@ -53,15 +53,17 @@ def tile_p_a_gin_kernel(tc, table, w_nb, w_self, b, dist, score, offs, out):
 
         banks = [(c, k) for c in range(CHUNKS) for k in range(BLOCKS)]
 
-        scaled = {}
+        d = [held.tile([P, CHUNK_NODES, ANCHORS], F32, name=f"d{c}") for c in range(CHUNKS)]
         for c in range(CHUNKS):
-            d = work.tile([P, CHUNK_NODES, ANCHORS], F32, name="d")
             nc.vector.tensor_tensor(
-                d[:],
+                d[c][:],
                 dist_sb[c][:].rearrange("p (n a) -> p n a", a=ANCHORS),
                 score_sb[:].unsqueeze(1).to_broadcast([P, CHUNK_NODES, ANCHORS]),
                 MULT,
             )
+
+        scaled = {}
+        for c in range(CHUNKS):
             for k in range(BLOCKS):
                 bank = psum.tile([P, CHUNK], F32, name="bank")
                 for half in range(CHUNK // PIECE):
@@ -74,17 +76,17 @@ def tile_p_a_gin_kernel(tc, table, w_nb, w_self, b, dist, score, offs, out):
                         stop=True,
                     )
                 scaled[c, k] = held.tile([P, CHUNK_NODES, ANCHORS], F32, name=f"scaled{c}_{k}")
-                nc.vector.tensor_tensor(scaled[c, k][:], bank[:].rearrange("p (n a) -> p n a", a=ANCHORS), d[:], MULT)
+                nc.vector.tensor_tensor(scaled[c, k][:], bank[:].rearrange("p (n a) -> p n a", a=ANCHORS), d[c][:], MULT)
 
         summed = {}
         for c, k in banks:
             nodes = slice(c * CHUNK_NODES, (c + 1) * CHUNK_NODES)
             summed[c, k] = held.tile([P, CHUNK_NODES, ANCHORS], F32, name=f"summed{c}_{k}")
-            engine = nc.vector if c == VECTOR_CHUNK else nc.gpsimd
+            engine, own = (nc.vector, own_ps[k]) if c == VECTOR_CHUNK else (nc.gpsimd, own_sb[k])
             engine.tensor_tensor(
                 summed[c, k][:],
                 scaled[c, k][:],
-                own_sb[k][:, nodes].unsqueeze(2).to_broadcast([P, CHUNK_NODES, ANCHORS]),
+                own[:, nodes].unsqueeze(2).to_broadcast([P, CHUNK_NODES, ANCHORS]),
                 ADD,
             )
 

@@ -1,4 +1,5 @@
 import concourse.mybir as mybir
+from concourse.masks import make_identity
 
 BF16, F32, U16 = mybir.dt.bfloat16, mybir.dt.float32, mybir.dt.uint16
 MULT, ADD = mybir.AluOpType.mult, mybir.AluOpType.add
@@ -14,7 +15,9 @@ PIECE_COLS = PIECE // 16
 CHUNK = 512
 CHUNKS = ENTRIES // CHUNK
 CHUNK_NODES = CHUNK // ANCHORS
-VECTOR_CHUNK = CHUNKS - 2
+PSUM_BANKS = 8
+TENSOR_CHUNK = CHUNKS - 1
+VECTOR_BANK = (CHUNKS - 2, BLOCKS - 1)
 
 FLOPS = 2 * P * (BLOCKS * P) * (ENTRIES + NODES)
 
@@ -23,9 +26,7 @@ def tile_p_a_gin_kernel(tc, table, w_nb, w_self, b, dist, score, offs, out):
     nc = tc.nc
     with (
         tc.tile_pool(name="held", bufs=1) as held,
-        tc.tile_pool(name="work", bufs=4) as work,
-        tc.psum_pool(name="kept", bufs=1) as kept,
-        tc.psum_pool(name="psum", bufs=6) as psum,
+        tc.psum_pool(name="psum", bufs=PSUM_BANKS) as psum,
     ):
         offsets = held.tile([P, ENTRIES // 16], U16, name="offsets")
         nc.sync.dma_start(offsets[:], offs)
@@ -45,11 +46,16 @@ def tile_p_a_gin_kernel(tc, table, w_nb, w_self, b, dist, score, offs, out):
         for k in range(BLOCKS):
             nc.sync.dma_start(b_sb[k][:], b[k * P : (k + 1) * P, :])
 
-        own_ps = [kept.tile([P, NODES], F32, name=f"own_ps{k}") for k in range(BLOCKS)]
+        ident = held.tile([P, P], F32, name="ident")
+        make_identity(nc, ident[:])
+
+
+        own_ps = psum.tile([P, BLOCKS, NODES], F32, name="own_ps", tag="bank")
         own_sb = [held.tile([P, NODES], F32, name=f"own_sb{k}") for k in range(BLOCKS)]
         for k in range(BLOCKS):
-            nc.tensor.matmul(own_ps[k][:], w_self_sb[:, k * P : (k + 1) * P], table_sb[:], start=True, stop=True)
-            nc.scalar.copy(own_sb[k][:], own_ps[k][:])
+            nc.tensor.matmul(own_ps[:, k, :], w_self_sb[:, k * P : (k + 1) * P], table_sb[:], start=True, stop=True)
+        for k in range(BLOCKS):
+            nc.scalar.copy(own_sb[k][:], own_ps[:, k, :])
 
         banks = [(c, k) for c in range(CHUNKS) for k in range(BLOCKS)]
 
@@ -65,7 +71,7 @@ def tile_p_a_gin_kernel(tc, table, w_nb, w_self, b, dist, score, offs, out):
         scaled = {}
         for c in range(CHUNKS):
             for k in range(BLOCKS):
-                bank = psum.tile([P, CHUNK], F32, name="bank")
+                bank = psum.tile([P, CHUNK], F32, name="bank", tag="bank")
                 for half in range(CHUNK // PIECE):
                     piece = c * (CHUNK // PIECE) + half
                     nc.tensor.matmul(
@@ -81,22 +87,41 @@ def tile_p_a_gin_kernel(tc, table, w_nb, w_self, b, dist, score, offs, out):
         summed = {}
         for c, k in banks:
             nodes = slice(c * CHUNK_NODES, (c + 1) * CHUNK_NODES)
-            summed[c, k] = held.tile([P, CHUNK_NODES, ANCHORS], F32, name=f"summed{c}_{k}")
-            engine, own = (nc.vector, own_ps[k]) if c == VECTOR_CHUNK else (nc.gpsimd, own_sb[k])
-            engine.tensor_tensor(
-                summed[c, k][:],
-                scaled[c, k][:],
-                own[:, nodes].unsqueeze(2).to_broadcast([P, CHUNK_NODES, ANCHORS]),
-                ADD,
-            )
+            if c == TENSOR_CHUNK:
+                summed[c, k] = psum.tile([P, CHUNK_NODES, ANCHORS], F32, name=f"summed{c}_{k}", tag="bank")
+                nc.tensor.matmul(summed[c, k][:], ident[:], scaled[c, k][:], start=True, stop=False)
+                nc.tensor.matmul(
+                    summed[c, k][:],
+                    w_self_sb[:, k * P : (k + 1) * P],
+                    table_sb[:, nodes].unsqueeze(2).to_broadcast([P, CHUNK_NODES, ANCHORS]),
+                    start=False,
+                    stop=True,
+                )
+            elif (c, k) == VECTOR_BANK:
+                summed[c, k] = held.tile([P, CHUNK_NODES, ANCHORS], F32, name=f"summed{c}_{k}")
+                nc.vector.tensor_tensor(
+                    summed[c, k][:],
+                    scaled[c, k][:],
+                    own_ps[:, k, nodes].unsqueeze(2).to_broadcast([P, CHUNK_NODES, ANCHORS]),
+                    ADD,
+                )
+            else:
+                summed[c, k] = held.tile([P, CHUNK_NODES, ANCHORS], F32, name=f"summed{c}_{k}")
+                nc.gpsimd.tensor_tensor(
+                    summed[c, k][:],
+                    scaled[c, k][:],
+                    own_sb[k][:, nodes].unsqueeze(2).to_broadcast([P, CHUNK_NODES, ANCHORS]),
+                    ADD,
+                )
 
         b_mean = [held.tile([P, 1], F32, name=f"b_mean{k}") for k in range(BLOCKS)]
         for k in range(BLOCKS):
             nc.scalar.mul(b_mean[k][:], b_sb[k][:], 1.0 / ANCHORS)
         mean = [held.tile([P, NODES], F32, name=f"mean{k}") for k in range(BLOCKS)]
-        for c, k in banks:
+        gpsimd_last = (VECTOR_BANK[0], VECTOR_BANK[1] - 1)
+        for c, k in [bank for bank in banks if bank != gpsimd_last] + [gpsimd_last]:
             nodes = slice(c * CHUNK_NODES, (c + 1) * CHUNK_NODES)
-            hidden = work.tile([P, CHUNK_NODES, ANCHORS], F32, name="hidden")
+            hidden = held.tile([P, CHUNK_NODES, ANCHORS], F32, name=f"hidden{c}_{k}")
             nc.scalar.activation(hidden[:], summed[c, k][:], RELU, bias=b_mean[k][:], scale=1.0 / ANCHORS)
             nc.vector.tensor_reduce(mean[k][:, nodes], hidden[:], axis=mybir.AxisListType.X, op=ADD)
 

@@ -16,8 +16,7 @@ CHUNK = 512
 CHUNKS = ENTRIES // CHUNK
 CHUNK_NODES = CHUNK // ANCHORS
 PSUM_BANKS = 8
-TENSOR_CHUNK = CHUNKS - 1
-VECTOR_BANK = (CHUNKS - 2, BLOCKS - 1)
+TENSOR_CHUNK = CHUNKS - 2
 
 FLOPS = 2 * P * (BLOCKS * P) * (ENTRIES + NODES)
 
@@ -36,8 +35,8 @@ def tile_p_a_gin_kernel(tc, table, w_nb, w_self, b, dist, score, offs, out):
         nc.sync.dma_start(w_nb_sb[:], w_nb)
         w_self_sb = held.tile([P, BLOCKS * P], BF16, name="w_self_sb")
         nc.scalar.dma_start(w_self_sb[:], w_self)
-        score_sb = held.tile([P, ANCHORS], F32, name="score_sb")
-        nc.scalar.dma_start(score_sb[:], score.broadcast_to([P, ANCHORS]))
+        score_row = held.tile([1, ANCHORS], F32, name="score_row")
+        nc.scalar.dma_start(score_row[:], score)
         dist_sb = [held.tile([P, CHUNK], F32, name=f"dist_sb{c}") for c in range(CHUNKS)]
         for c in range(CHUNKS):
             queue = nc.scalar if c % 2 == 0 else nc.sync
@@ -57,19 +56,22 @@ def tile_p_a_gin_kernel(tc, table, w_nb, w_self, b, dist, score, offs, out):
         for k in range(BLOCKS):
             nc.scalar.copy(own_sb[k][:], own_ps[:, k, :])
 
-        banks = [(c, k) for c in range(CHUNKS) for k in range(BLOCKS)]
+        ones_row = held.tile([1, P], F32, name="ones_row")
+        nc.vector.memset(ones_row[:], 1.0)
+        score_ps = psum.tile([P, ANCHORS], F32, name="score_ps", tag="bank")
+        nc.tensor.matmul(score_ps[:], ones_row[:], score_row[:], start=True, stop=True)
 
-        d = [held.tile([P, CHUNK_NODES, ANCHORS], F32, name=f"d{c}") for c in range(CHUNKS)]
-        for c in range(CHUNKS):
-            nc.vector.tensor_tensor(
-                d[c][:],
-                dist_sb[c][:].rearrange("p (n a) -> p n a", a=ANCHORS),
-                score_sb[:].unsqueeze(1).to_broadcast([P, CHUNK_NODES, ANCHORS]),
-                MULT,
-            )
+        banks = [(c, k) for c in range(CHUNKS) for k in range(BLOCKS)]
 
         scaled = {}
         for c in range(CHUNKS):
+            d = held.tile([P, CHUNK_NODES, ANCHORS], F32, name=f"d{c}")
+            nc.vector.tensor_tensor(
+                d[:],
+                dist_sb[c][:].rearrange("p (n a) -> p n a", a=ANCHORS),
+                score_ps[:].unsqueeze(1).to_broadcast([P, CHUNK_NODES, ANCHORS]),
+                MULT,
+            )
             for k in range(BLOCKS):
                 bank = psum.tile([P, CHUNK], F32, name="bank", tag="bank")
                 for half in range(CHUNK // PIECE):
@@ -82,7 +84,7 @@ def tile_p_a_gin_kernel(tc, table, w_nb, w_self, b, dist, score, offs, out):
                         stop=True,
                     )
                 scaled[c, k] = held.tile([P, CHUNK_NODES, ANCHORS], F32, name=f"scaled{c}_{k}")
-                nc.vector.tensor_tensor(scaled[c, k][:], bank[:].rearrange("p (n a) -> p n a", a=ANCHORS), d[c][:], MULT)
+                nc.vector.tensor_tensor(scaled[c, k][:], bank[:].rearrange("p (n a) -> p n a", a=ANCHORS), d[:], MULT)
 
         summed = {}
         for c, k in banks:
@@ -97,14 +99,6 @@ def tile_p_a_gin_kernel(tc, table, w_nb, w_self, b, dist, score, offs, out):
                     start=False,
                     stop=True,
                 )
-            elif (c, k) == VECTOR_BANK:
-                summed[c, k] = held.tile([P, CHUNK_NODES, ANCHORS], F32, name=f"summed{c}_{k}")
-                nc.vector.tensor_tensor(
-                    summed[c, k][:],
-                    scaled[c, k][:],
-                    own_ps[:, k, nodes].unsqueeze(2).to_broadcast([P, CHUNK_NODES, ANCHORS]),
-                    ADD,
-                )
             else:
                 summed[c, k] = held.tile([P, CHUNK_NODES, ANCHORS], F32, name=f"summed{c}_{k}")
                 nc.gpsimd.tensor_tensor(
@@ -118,8 +112,8 @@ def tile_p_a_gin_kernel(tc, table, w_nb, w_self, b, dist, score, offs, out):
         for k in range(BLOCKS):
             nc.scalar.mul(b_mean[k][:], b_sb[k][:], 1.0 / ANCHORS)
         mean = [held.tile([P, NODES], F32, name=f"mean{k}") for k in range(BLOCKS)]
-        gpsimd_last = (VECTOR_BANK[0], VECTOR_BANK[1] - 1)
-        for c, k in [bank for bank in banks if bank != gpsimd_last] + [gpsimd_last]:
+        in_turn = [(c, k) for k in range(BLOCKS) for c in (TENSOR_CHUNK, TENSOR_CHUNK + 1)]
+        for c, k in banks[: TENSOR_CHUNK * BLOCKS] + in_turn:
             nodes = slice(c * CHUNK_NODES, (c + 1) * CHUNK_NODES)
             hidden = held.tile([P, CHUNK_NODES, ANCHORS], F32, name=f"hidden{c}_{k}")
             nc.scalar.activation(hidden[:], summed[c, k][:], RELU, bias=b_mean[k][:], scale=1.0 / ANCHORS)

@@ -1,5 +1,4 @@
 import concourse.mybir as mybir
-from concourse.masks import make_identity
 
 BF16, F32, U16 = mybir.dt.bfloat16, mybir.dt.float32, mybir.dt.uint16
 MULT, ADD = mybir.AluOpType.mult, mybir.AluOpType.add
@@ -16,7 +15,7 @@ CHUNK = 512
 CHUNKS = ENTRIES // CHUNK
 CHUNK_NODES = CHUNK // ANCHORS
 PSUM_BANKS = 8
-TENSOR_CHUNK = CHUNKS - 2
+VECTOR_CHUNK = CHUNKS - 2
 
 FLOPS = 2 * P * (BLOCKS * P) * (ENTRIES + NODES)
 
@@ -44,9 +43,6 @@ def tile_p_a_gin_kernel(tc, table, w_nb, w_self, b, dist, score, offs, out):
         b_sb = [held.tile([P, 1], F32, name=f"b_sb{k}") for k in range(BLOCKS)]
         for k in range(BLOCKS):
             nc.sync.dma_start(b_sb[k][:], b[k * P : (k + 1) * P, :])
-
-        ident = held.tile([P, P], F32, name="ident")
-        make_identity(nc, ident[:])
 
 
         own_ps = psum.tile([P, BLOCKS, NODES], F32, name="own_ps", tag="bank")
@@ -89,15 +85,13 @@ def tile_p_a_gin_kernel(tc, table, w_nb, w_self, b, dist, score, offs, out):
         summed = {}
         for c, k in banks:
             nodes = slice(c * CHUNK_NODES, (c + 1) * CHUNK_NODES)
-            if c == TENSOR_CHUNK:
-                summed[c, k] = psum.tile([P, CHUNK_NODES, ANCHORS], F32, name=f"summed{c}_{k}", tag="bank")
-                nc.tensor.matmul(summed[c, k][:], ident[:], scaled[c, k][:], start=True, stop=False)
-                nc.tensor.matmul(
+            if c == VECTOR_CHUNK:
+                summed[c, k] = held.tile([P, CHUNK_NODES, ANCHORS], F32, name=f"summed{c}_{k}")
+                nc.vector.tensor_tensor(
                     summed[c, k][:],
-                    w_self_sb[:, k * P : (k + 1) * P],
-                    table_sb[:, nodes].unsqueeze(2).to_broadcast([P, CHUNK_NODES, ANCHORS]),
-                    start=False,
-                    stop=True,
+                    scaled[c, k][:],
+                    own_ps[:, k, nodes].unsqueeze(2).to_broadcast([P, CHUNK_NODES, ANCHORS]),
+                    ADD,
                 )
             else:
                 summed[c, k] = held.tile([P, CHUNK_NODES, ANCHORS], F32, name=f"summed{c}_{k}")
@@ -112,8 +106,7 @@ def tile_p_a_gin_kernel(tc, table, w_nb, w_self, b, dist, score, offs, out):
         for k in range(BLOCKS):
             nc.scalar.mul(b_mean[k][:], b_sb[k][:], 1.0 / ANCHORS)
         mean = [held.tile([P, NODES], F32, name=f"mean{k}") for k in range(BLOCKS)]
-        in_turn = [(c, k) for k in range(BLOCKS) for c in (TENSOR_CHUNK, TENSOR_CHUNK + 1)]
-        for c, k in banks[: TENSOR_CHUNK * BLOCKS] + in_turn:
+        for c, k in banks:
             nodes = slice(c * CHUNK_NODES, (c + 1) * CHUNK_NODES)
             hidden = held.tile([P, CHUNK_NODES, ANCHORS], F32, name=f"hidden{c}_{k}")
             nc.scalar.activation(hidden[:], summed[c, k][:], RELU, bias=b_mean[k][:], scale=1.0 / ANCHORS)

@@ -15,6 +15,7 @@ CHUNK = 512
 CHUNKS = ENTRIES // CHUNK
 CHUNK_NODES = CHUNK // ANCHORS
 PSUM_BANKS = 8
+EARLY_D = 2
 VECTOR_CHUNK = CHUNKS - 2
 
 FLOPS = 2 * P * (BLOCKS * P) * (ENTRIES + NODES)
@@ -26,24 +27,28 @@ def tile_p_a_gin_kernel(tc, table, w_nb, w_self, b, dist, score, offs, out):
         tc.tile_pool(name="held", bufs=1) as held,
         tc.psum_pool(name="psum", bufs=PSUM_BANKS) as psum,
     ):
-        offsets = held.tile([P, ENTRIES // 16], U16, name="offsets")
-        nc.sync.dma_start(offsets[:], offs)
-        table_sb = held.tile([P, NODES], BF16, name="table_sb")
-        nc.sync.dma_start(table_sb[:], table)
-        w_nb_sb = held.tile([P, BLOCKS * P], BF16, name="w_nb_sb")
-        nc.sync.dma_start(w_nb_sb[:], w_nb)
-        w_self_sb = held.tile([P, BLOCKS * P], BF16, name="w_self_sb")
-        nc.scalar.dma_start(w_self_sb[:], w_self)
         score_row = held.tile([1, ANCHORS], F32, name="score_row")
         nc.scalar.dma_start(score_row[:], score)
+        table_sb = held.tile([P, NODES], BF16, name="table_sb")
+        nc.sync.dma_start(table_sb[:], table)
+        w_self_sb = held.tile([P, BLOCKS * P], BF16, name="w_self_sb")
+        nc.sync.dma_start(w_self_sb[:], w_self)
+        offsets = held.tile([P, ENTRIES // 16], U16, name="offsets")
+        nc.sync.dma_start(offsets[:], offs)
+        w_nb_sb = held.tile([P, BLOCKS * P], BF16, name="w_nb_sb")
+        nc.sync.dma_start(w_nb_sb[:], w_nb)
         dist_sb = [held.tile([P, CHUNK], F32, name=f"dist_sb{c}") for c in range(CHUNKS)]
         for c in range(CHUNKS):
-            queue = nc.scalar if c % 2 == 0 else nc.sync
+            queue = nc.scalar if c == 0 else nc.sync
             queue.dma_start(dist_sb[c][:], dist[:, c * CHUNK : (c + 1) * CHUNK].broadcast_to([P, CHUNK]))
-        b_sb = [held.tile([P, 1], F32, name=f"b_sb{k}") for k in range(BLOCKS)]
-        for k in range(BLOCKS):
-            nc.sync.dma_start(b_sb[k][:], b[k * P : (k + 1) * P, :])
+        b_sb = held.tile([P, BLOCKS], F32, name="b_sb")
+        nc.sync.dma_start(b_sb[:], b.rearrange("(k p) o -> p (k o)", p=P))
 
+
+        ones_row = held.tile([1, P], F32, name="ones_row")
+        nc.vector.memset(ones_row[:], 1.0)
+        score_ps = psum.tile([P, ANCHORS], F32, name="score_ps", tag="bank")
+        nc.tensor.matmul(score_ps[:], ones_row[:], score_row[:], start=True, stop=True)
 
         own_ps = psum.tile([P, BLOCKS, NODES], F32, name="own_ps", tag="bank")
         own_sb = [held.tile([P, NODES], F32, name=f"own_sb{k}") for k in range(BLOCKS)]
@@ -52,22 +57,18 @@ def tile_p_a_gin_kernel(tc, table, w_nb, w_self, b, dist, score, offs, out):
         for k in range(BLOCKS):
             nc.scalar.copy(own_sb[k][:], own_ps[:, k, :])
 
-        ones_row = held.tile([1, P], F32, name="ones_row")
-        nc.vector.memset(ones_row[:], 1.0)
-        score_ps = psum.tile([P, ANCHORS], F32, name="score_ps", tag="bank")
-        nc.tensor.matmul(score_ps[:], ones_row[:], score_row[:], start=True, stop=True)
-
         banks = [(c, k) for c in range(CHUNKS) for k in range(BLOCKS)]
 
-        scaled = {}
+        d, scaled = {}, {}
         for c in range(CHUNKS):
-            d = held.tile([P, CHUNK_NODES, ANCHORS], F32, name=f"d{c}")
-            nc.vector.tensor_tensor(
-                d[:],
-                dist_sb[c][:].rearrange("p (n a) -> p n a", a=ANCHORS),
-                score_ps[:].unsqueeze(1).to_broadcast([P, CHUNK_NODES, ANCHORS]),
-                MULT,
-            )
+            for ahead in range(EARLY_D) if c == 0 else range(c + EARLY_D - 1, min(c + EARLY_D, CHUNKS)):
+                d[ahead] = held.tile([P, CHUNK_NODES, ANCHORS], F32, name=f"d{ahead}")
+                nc.vector.tensor_tensor(
+                    d[ahead][:],
+                    dist_sb[ahead][:].rearrange("p (n a) -> p n a", a=ANCHORS),
+                    score_ps[:].unsqueeze(1).to_broadcast([P, CHUNK_NODES, ANCHORS]),
+                    MULT,
+                )
             for k in range(BLOCKS):
                 bank = psum.tile([P, CHUNK], F32, name="bank", tag="bank")
                 for half in range(CHUNK // PIECE):
@@ -80,7 +81,7 @@ def tile_p_a_gin_kernel(tc, table, w_nb, w_self, b, dist, score, offs, out):
                         stop=True,
                     )
                 scaled[c, k] = held.tile([P, CHUNK_NODES, ANCHORS], F32, name=f"scaled{c}_{k}")
-                nc.vector.tensor_tensor(scaled[c, k][:], bank[:].rearrange("p (n a) -> p n a", a=ANCHORS), d[:], MULT)
+                nc.vector.tensor_tensor(scaled[c, k][:], bank[:].rearrange("p (n a) -> p n a", a=ANCHORS), d[c][:], MULT)
 
         summed = {}
         for c, k in banks:
@@ -102,14 +103,13 @@ def tile_p_a_gin_kernel(tc, table, w_nb, w_self, b, dist, score, offs, out):
                     ADD,
                 )
 
-        b_mean = [held.tile([P, 1], F32, name=f"b_mean{k}") for k in range(BLOCKS)]
-        for k in range(BLOCKS):
-            nc.scalar.mul(b_mean[k][:], b_sb[k][:], 1.0 / ANCHORS)
+        b_mean = held.tile([P, BLOCKS], F32, name="b_mean")
+        nc.scalar.mul(b_mean[:], b_sb[:], 1.0 / ANCHORS)
         mean = [held.tile([P, NODES], F32, name=f"mean{k}") for k in range(BLOCKS)]
         for c, k in banks:
             nodes = slice(c * CHUNK_NODES, (c + 1) * CHUNK_NODES)
             hidden = held.tile([P, CHUNK_NODES, ANCHORS], F32, name=f"hidden{c}_{k}")
-            nc.scalar.activation(hidden[:], summed[c, k][:], RELU, bias=b_mean[k][:], scale=1.0 / ANCHORS)
+            nc.scalar.activation(hidden[:], summed[c, k][:], RELU, bias=b_mean[:, k : k + 1], scale=1.0 / ANCHORS)
             nc.vector.tensor_reduce(mean[k][:, nodes], hidden[:], axis=mybir.AxisListType.X, op=ADD)
 
         for k in range(BLOCKS):

@@ -1,7 +1,7 @@
 import concourse.mybir as mybir
 
 BF16, F32, U16 = mybir.dt.bfloat16, mybir.dt.float32, mybir.dt.uint16
-MULT, ADD = mybir.AluOpType.mult, mybir.AluOpType.add
+MULT, ADD, SUB = mybir.AluOpType.mult, mybir.AluOpType.add, mybir.AluOpType.subtract
 RELU = mybir.ActivationFunctionType.Relu
 
 P = 128
@@ -15,10 +15,17 @@ CHUNK = 512
 CHUNKS = ENTRIES // CHUNK
 CHUNK_NODES = CHUNK // ANCHORS
 PSUM_BANKS = 8
-EARLY_D = 2
-VECTOR_CHUNK = CHUNKS - 2
+GPSIMD_BANKS = 5
+ROW = 64
+ROWS = ENTRIES // ROW
+ROWS_PER_CHUNK = CHUNK // ROW
+PARTS = 3
 
 FLOPS = 2 * P * (BLOCKS * P) * (ENTRIES + NODES)
+
+
+def leading_part(ap):
+    return ap.bitcast(BF16).rearrange("p (n two) -> p n two", two=2)[:, :, 1]
 
 
 def tile_p_a_gin_kernel(tc, table, w_nb, w_self, b, dist, score, offs, out):
@@ -27,66 +34,88 @@ def tile_p_a_gin_kernel(tc, table, w_nb, w_self, b, dist, score, offs, out):
         tc.tile_pool(name="held", bufs=1) as held,
         tc.psum_pool(name="psum", bufs=PSUM_BANKS) as psum,
     ):
-        score_row = held.tile([1, ANCHORS], F32, name="score_row")
-        nc.scalar.dma_start(score_row[:], score)
+        dist_rows = held.tile([PARTS * ROWS, ROW], F32, name="dist_rows")
+        for g in range(PARTS):
+            nc.sync.dma_start(dist_rows[g * ROWS : (g + 1) * ROWS, :], dist.rearrange("o (q n) -> (o q) n", q=ROWS))
+        score_sb = held.tile([P, ANCHORS], F32, name="score_sb")
+        nc.scalar.dma_start(score_sb[:], score.broadcast_to([P, ANCHORS]))
         table_sb = held.tile([P, NODES], BF16, name="table_sb")
         nc.sync.dma_start(table_sb[:], table)
         w_self_sb = held.tile([P, BLOCKS * P], BF16, name="w_self_sb")
-        nc.sync.dma_start(w_self_sb[:], w_self)
+        nc.scalar.dma_start(w_self_sb[:], w_self)
         offsets = held.tile([P, ENTRIES // 16], U16, name="offsets")
         nc.sync.dma_start(offsets[:], offs)
         w_nb_sb = held.tile([P, BLOCKS * P], BF16, name="w_nb_sb")
-        nc.sync.dma_start(w_nb_sb[:], w_nb)
-        dist_sb = [held.tile([P, CHUNK], F32, name=f"dist_sb{c}") for c in range(CHUNKS)]
-        for c in range(CHUNKS):
-            queue = nc.scalar if c == 0 else nc.sync
-            queue.dma_start(dist_sb[c][:], dist[:, c * CHUNK : (c + 1) * CHUNK].broadcast_to([P, CHUNK]))
+        nc.scalar.dma_start(w_nb_sb[:], w_nb)
         b_sb = held.tile([P, BLOCKS], F32, name="b_sb")
-        nc.sync.dma_start(b_sb[:], b.rearrange("(k p) o -> p (k o)", p=P))
+        nc.gpsimd.dma_start(b_sb[:], b.rearrange("(k p) o -> p (k o)", p=P))
 
+        ones = held.tile([P, ROWS], F32, name="ones")
+        nc.vector.memset(ones[:], 1.0)
+        count_columns = held.tile([P, ROWS], F32, name="count_columns", align_bytes=64)
+        nc.vector.tensor_tensor_scan(count_columns[:], ones[:], ones[:], 0.0, MULT, ADD)
+        count_rows = held.tile([P, ROWS], F32, name="count_rows", align_bytes=64)
+        nc.vector.transpose(count_rows[:], count_columns[:])
+        pick = held.tile([P, ROWS], BF16, name="pick")
+        nc.vector.tensor_tensor(pick[:], count_rows[:], count_columns[:], mybir.AluOpType.is_equal)
 
-        ones_row = held.tile([1, P], F32, name="ones_row")
-        nc.vector.memset(ones_row[:], 1.0)
-        score_ps = psum.tile([P, ANCHORS], F32, name="score_ps", tag="bank")
-        nc.tensor.matmul(score_ps[:], ones_row[:], score_row[:], start=True, stop=True)
+        parts = held.tile([P, ROW], F32, name="parts")
+        nc.vector.memset(parts[PARTS * ROWS :, :], 0.0)
+        nc.vector.tensor_tensor(
+            parts[: PARTS * ROWS, :].rearrange("p (n a) -> p n a", a=ANCHORS),
+            dist_rows[:].rearrange("p (n a) -> p n a", a=ANCHORS),
+            score_sb[: PARTS * ROWS, :].unsqueeze(1).to_broadcast([PARTS * ROWS, ROW // ANCHORS, ANCHORS]),
+            MULT,
+        )
+        for rows in (2 * ROWS, ROWS):
+            nc.vector.tensor_tensor(parts[:rows, :], parts[:rows, :], leading_part(parts[:rows, :]), SUB)
+
 
         own_ps = psum.tile([P, BLOCKS, NODES], F32, name="own_ps", tag="bank")
         own_sb = [held.tile([P, NODES], F32, name=f"own_sb{k}") for k in range(BLOCKS)]
         for k in range(BLOCKS):
             nc.tensor.matmul(own_ps[:, k, :], w_self_sb[:, k * P : (k + 1) * P], table_sb[:], start=True, stop=True)
+
+        d = [held.tile([P, CHUNK_NODES, ANCHORS], F32, name=f"d{c}") for c in range(CHUNKS)]
+        d_ps = [psum.tile([P, CHUNK], F32, name=f"d_ps{c}", tag="bank") for c in range(CHUNKS)]
+        for c in range(CHUNKS):
+            for i in range(ROWS_PER_CHUNK):
+                q = c * ROWS_PER_CHUNK + i
+                nc.tensor.matmul(
+                    d_ps[c][:, i * ROW : (i + 1) * ROW],
+                    pick[:, q : q + 1].to_broadcast([P, P]),
+                    leading_part(parts[:]),
+                    start=True,
+                    stop=True,
+                )
+        nc.scalar.copy(d[0][:].rearrange("p n a -> p (n a)"), d_ps[0][:])
         for k in range(BLOCKS):
             nc.scalar.copy(own_sb[k][:], own_ps[:, k, :])
+        for c in range(1, CHUNKS):
+            nc.scalar.copy(d[c][:].rearrange("p n a -> p (n a)"), d_ps[c][:])
 
         banks = [(c, k) for c in range(CHUNKS) for k in range(BLOCKS)]
-
-        d, scaled = {}, {}
-        for c in range(CHUNKS):
-            for ahead in range(EARLY_D) if c == 0 else range(c + EARLY_D - 1, min(c + EARLY_D, CHUNKS)):
-                d[ahead] = held.tile([P, CHUNK_NODES, ANCHORS], F32, name=f"d{ahead}")
-                nc.vector.tensor_tensor(
-                    d[ahead][:],
-                    dist_sb[ahead][:].rearrange("p (n a) -> p n a", a=ANCHORS),
-                    score_ps[:].unsqueeze(1).to_broadcast([P, CHUNK_NODES, ANCHORS]),
-                    MULT,
+        scaled = {}
+        for c, k in banks:
+            bank = psum.tile([P, CHUNK], F32, name="bank", tag="bank")
+            for half in range(CHUNK // PIECE):
+                piece = c * (CHUNK // PIECE) + half
+                nc.tensor.matmul(
+                    bank[:, half * PIECE : (half + 1) * PIECE],
+                    w_nb_sb[:, k * P : (k + 1) * P],
+                    table_sb[:].indirect(offsets[:, piece * PIECE_COLS : (piece + 1) * PIECE_COLS]),
+                    start=True,
+                    stop=True,
                 )
-            for k in range(BLOCKS):
-                bank = psum.tile([P, CHUNK], F32, name="bank", tag="bank")
-                for half in range(CHUNK // PIECE):
-                    piece = c * (CHUNK // PIECE) + half
-                    nc.tensor.matmul(
-                        bank[:, half * PIECE : (half + 1) * PIECE],
-                        w_nb_sb[:, k * P : (k + 1) * P],
-                        table_sb[:].indirect(offsets[:, piece * PIECE_COLS : (piece + 1) * PIECE_COLS]),
-                        start=True,
-                        stop=True,
-                    )
-                scaled[c, k] = held.tile([P, CHUNK_NODES, ANCHORS], F32, name=f"scaled{c}_{k}")
-                nc.vector.tensor_tensor(scaled[c, k][:], bank[:].rearrange("p (n a) -> p n a", a=ANCHORS), d[c][:], MULT)
+            scaled[c, k] = held.tile([P, CHUNK_NODES, ANCHORS], F32, name=f"scaled{c}_{k}")
+            nc.vector.tensor_tensor(
+                scaled[c, k][:], bank[:].rearrange("p (n a) -> p n a", a=ANCHORS), d[c][:], MULT
+            )
 
         summed = {}
-        for c, k in banks:
+        for i, (c, k) in enumerate(banks):
             nodes = slice(c * CHUNK_NODES, (c + 1) * CHUNK_NODES)
-            if c == VECTOR_CHUNK:
+            if i >= GPSIMD_BANKS:
                 summed[c, k] = held.tile([P, CHUNK_NODES, ANCHORS], F32, name=f"summed{c}_{k}")
                 nc.vector.tensor_tensor(
                     summed[c, k][:],

@@ -1,4 +1,5 @@
 import concourse.mybir as mybir
+from concourse.masks import make_identity
 
 BF16, F32, U16 = mybir.dt.bfloat16, mybir.dt.float32, mybir.dt.uint16
 MULT, ADD, SUB = mybir.AluOpType.mult, mybir.AluOpType.add, mybir.AluOpType.subtract
@@ -14,8 +15,9 @@ PIECE_COLS = PIECE // 16
 CHUNK = 512
 CHUNKS = ENTRIES // CHUNK
 CHUNK_NODES = CHUNK // ANCHORS
-PSUM_BANKS = 8
-GPSIMD_BANKS = 5
+LOOKUP_BANKS = 4
+D_BANKS = 3
+TENSOR_CHUNK = CHUNKS - 2
 ROW = 64
 ROWS = ENTRIES // ROW
 ROWS_PER_CHUNK = CHUNK // ROW
@@ -32,7 +34,9 @@ def tile_p_a_gin_kernel(tc, table, w_nb, w_self, b, dist, score, offs, out):
     nc = tc.nc
     with (
         tc.tile_pool(name="held", bufs=1) as held,
-        tc.psum_pool(name="psum", bufs=PSUM_BANKS) as psum,
+        tc.psum_pool(name="psum_own", bufs=1) as psum_own,
+        tc.psum_pool(name="psum_d", bufs=D_BANKS) as psum_d,
+        tc.psum_pool(name="psum", bufs=LOOKUP_BANKS) as psum,
     ):
         dist_rows = held.tile([PARTS * ROWS, ROW], F32, name="dist_rows")
         for g in range(PARTS):
@@ -70,34 +74,37 @@ def tile_p_a_gin_kernel(tc, table, w_nb, w_self, b, dist, score, offs, out):
         for rows in (2 * ROWS, ROWS):
             nc.vector.tensor_tensor(parts[:rows, :], parts[:rows, :], leading_part(parts[:rows, :]), SUB)
 
-
-        own_ps = psum.tile([P, BLOCKS, NODES], F32, name="own_ps", tag="bank")
+        own_ps = psum_own.tile([P, BLOCKS, NODES], F32, name="own_ps")
         own_sb = [held.tile([P, NODES], F32, name=f"own_sb{k}") for k in range(BLOCKS)]
         for k in range(BLOCKS):
             nc.tensor.matmul(own_ps[:, k, :], w_self_sb[:, k * P : (k + 1) * P], table_sb[:], start=True, stop=True)
 
         d = [held.tile([P, CHUNK_NODES, ANCHORS], F32, name=f"d{c}") for c in range(CHUNKS)]
-        d_ps = [psum.tile([P, CHUNK], F32, name=f"d_ps{c}", tag="bank") for c in range(CHUNKS)]
-        for c in range(CHUNKS):
+
+        def spread_d(c):
+            d_ps = psum_d.tile([P, CHUNK], F32, name="d_ps")
             for i in range(ROWS_PER_CHUNK):
                 q = c * ROWS_PER_CHUNK + i
                 nc.tensor.matmul(
-                    d_ps[c][:, i * ROW : (i + 1) * ROW],
+                    d_ps[:, i * ROW : (i + 1) * ROW],
                     pick[:, q : q + 1].to_broadcast([P, P]),
                     leading_part(parts[:]),
                     start=True,
                     stop=True,
                 )
-        nc.scalar.copy(d[0][:].rearrange("p n a -> p (n a)"), d_ps[0][:])
-        for k in range(BLOCKS):
-            nc.scalar.copy(own_sb[k][:], own_ps[:, k, :])
-        for c in range(1, CHUNKS):
-            nc.scalar.copy(d[c][:].rearrange("p n a -> p (n a)"), d_ps[c][:])
+            nc.scalar.copy(d[c][:].rearrange("p n a -> p (n a)"), d_ps[:])
 
         banks = [(c, k) for c in range(CHUNKS) for k in range(BLOCKS)]
         scaled = {}
         for c, k in banks:
-            bank = psum.tile([P, CHUNK], F32, name="bank", tag="bank")
+            if (c, k) == (0, 0):
+                spread_d(0)
+                for block in range(BLOCKS):
+                    nc.scalar.copy(own_sb[block][:], own_ps[:, block, :])
+            elif (c, k) == (1, 0):
+                for later in range(1, CHUNKS):
+                    spread_d(later)
+            bank = psum.tile([P, CHUNK], F32, name="bank")
             for half in range(CHUNK // PIECE):
                 piece = c * (CHUNK // PIECE) + half
                 nc.tensor.matmul(
@@ -112,16 +119,20 @@ def tile_p_a_gin_kernel(tc, table, w_nb, w_self, b, dist, score, offs, out):
                 scaled[c, k][:], bank[:].rearrange("p (n a) -> p n a", a=ANCHORS), d[c][:], MULT
             )
 
+        identity = held.tile([P, P], F32, name="identity")
+        make_identity(nc, identity[:])
         summed = {}
-        for i, (c, k) in enumerate(banks):
+        for c, k in banks:
             nodes = slice(c * CHUNK_NODES, (c + 1) * CHUNK_NODES)
-            if i >= GPSIMD_BANKS:
-                summed[c, k] = held.tile([P, CHUNK_NODES, ANCHORS], F32, name=f"summed{c}_{k}")
-                nc.vector.tensor_tensor(
+            if c == TENSOR_CHUNK:
+                summed[c, k] = psum_d.tile([P, CHUNK_NODES, ANCHORS], F32, name=f"summed{c}_{k}", tag="d_ps")
+                nc.tensor.matmul(summed[c, k][:], identity[:], scaled[c, k][:], start=True, stop=False)
+                nc.tensor.matmul(
                     summed[c, k][:],
-                    scaled[c, k][:],
-                    own_ps[:, k, nodes].unsqueeze(2).to_broadcast([P, CHUNK_NODES, ANCHORS]),
-                    ADD,
+                    w_self_sb[:, k * P : (k + 1) * P],
+                    table_sb[:, nodes].unsqueeze(2).to_broadcast([P, CHUNK_NODES, ANCHORS]),
+                    start=False,
+                    stop=True,
                 )
             else:
                 summed[c, k] = held.tile([P, CHUNK_NODES, ANCHORS], F32, name=f"summed{c}_{k}")

@@ -12,15 +12,14 @@ ENTRIES = NODES * ANCHORS
 BLOCKS = 2
 PIECE = NODES
 PIECE_COLS = PIECE // 16
-CHUNK = 512
-CHUNKS = ENTRIES // CHUNK
-CHUNK_NODES = CHUNK // ANCHORS
-LOOKUP_BANKS = 4
-D_BANKS = 3
-TENSOR_CHUNK = CHUNKS - 2
+BANK = 512
+HALF = BANK // 2
+CHUNKS = [(0, HALF)] + [(start, BANK) for start in range(HALF, ENTRIES - HALF, BANK)] + [(ENTRIES - HALF, HALF)]
+LOOKUP_BANKS = 3
+D_BANKS = 4
+TENSOR_CHUNK = len(CHUNKS) - 2
 ROW = 64
 ROWS = ENTRIES // ROW
-ROWS_PER_CHUNK = CHUNK // ROW
 PARTS = 3
 
 FLOPS = 2 * P * (BLOCKS * P) * (ENTRIES + NODES)
@@ -79,12 +78,16 @@ def tile_p_a_gin_kernel(tc, table, w_nb, w_self, b, dist, score, offs, out):
         for k in range(BLOCKS):
             nc.tensor.matmul(own_ps[:, k, :], w_self_sb[:, k * P : (k + 1) * P], table_sb[:], start=True, stop=True)
 
-        d = [held.tile([P, CHUNK_NODES, ANCHORS], F32, name=f"d{c}") for c in range(CHUNKS)]
+        d = {}
+
+        def by_node(ap):
+            return ap.rearrange("p (n a) -> p n a", a=ANCHORS)
 
         def spread_d(c):
-            d_ps = psum_d.tile([P, CHUNK], F32, name="d_ps")
-            for i in range(ROWS_PER_CHUNK):
-                q = c * ROWS_PER_CHUNK + i
+            start, size = CHUNKS[c]
+            d_ps = psum_d.tile([P, size], F32, name=f"d_ps{c}", tag="d_ps")
+            for i in range(size // ROW):
+                q = start // ROW + i
                 nc.tensor.matmul(
                     d_ps[:, i * ROW : (i + 1) * ROW],
                     pick[:, q : q + 1].to_broadcast([P, P]),
@@ -92,9 +95,10 @@ def tile_p_a_gin_kernel(tc, table, w_nb, w_self, b, dist, score, offs, out):
                     start=True,
                     stop=True,
                 )
-            nc.scalar.copy(d[c][:].rearrange("p n a -> p (n a)"), d_ps[:])
+            d[c] = held.tile([P, size], F32, name=f"d{c}")
+            nc.scalar.copy(d[c][:], d_ps[:])
 
-        banks = [(c, k) for c in range(CHUNKS) for k in range(BLOCKS)]
+        banks = [(c, k) for c in range(len(CHUNKS)) for k in range(BLOCKS)]
         scaled = {}
         for c, k in banks:
             if (c, k) == (0, 0):
@@ -102,44 +106,45 @@ def tile_p_a_gin_kernel(tc, table, w_nb, w_self, b, dist, score, offs, out):
                 for block in range(BLOCKS):
                     nc.scalar.copy(own_sb[block][:], own_ps[:, block, :])
             elif (c, k) == (1, 0):
-                for later in range(1, CHUNKS):
+                for later in range(1, len(CHUNKS)):
                     spread_d(later)
-            bank = psum.tile([P, CHUNK], F32, name="bank")
-            for half in range(CHUNK // PIECE):
-                piece = c * (CHUNK // PIECE) + half
+            start, size = CHUNKS[c]
+            bank = psum.tile([P, size], F32, name="bank", tag="bank")
+            for i in range(size // PIECE):
+                piece = start // PIECE + i
                 nc.tensor.matmul(
-                    bank[:, half * PIECE : (half + 1) * PIECE],
+                    bank[:, i * PIECE : (i + 1) * PIECE],
                     w_nb_sb[:, k * P : (k + 1) * P],
                     table_sb[:].indirect(offsets[:, piece * PIECE_COLS : (piece + 1) * PIECE_COLS]),
                     start=True,
                     stop=True,
                 )
-            scaled[c, k] = held.tile([P, CHUNK_NODES, ANCHORS], F32, name=f"scaled{c}_{k}")
-            nc.vector.tensor_tensor(
-                scaled[c, k][:], bank[:].rearrange("p (n a) -> p n a", a=ANCHORS), d[c][:], MULT
-            )
+            scaled[c, k] = held.tile([P, size], F32, name=f"scaled{c}_{k}")
+            nc.vector.tensor_tensor(scaled[c, k][:], bank[:], d[c][:], MULT)
 
         identity = held.tile([P, P], F32, name="identity")
         make_identity(nc, identity[:])
         summed = {}
         for c, k in banks:
-            nodes = slice(c * CHUNK_NODES, (c + 1) * CHUNK_NODES)
+            start, size = CHUNKS[c]
+            nodes = slice(start // ANCHORS, (start + size) // ANCHORS)
+            shape = [P, size // ANCHORS, ANCHORS]
             if c == TENSOR_CHUNK:
-                summed[c, k] = psum_d.tile([P, CHUNK_NODES, ANCHORS], F32, name=f"summed{c}_{k}", tag="d_ps")
+                summed[c, k] = psum_d.tile([P, size], F32, name=f"summed{c}_{k}", tag="d_ps")
                 nc.tensor.matmul(summed[c, k][:], identity[:], scaled[c, k][:], start=True, stop=False)
                 nc.tensor.matmul(
-                    summed[c, k][:],
+                    by_node(summed[c, k][:]),
                     w_self_sb[:, k * P : (k + 1) * P],
-                    table_sb[:, nodes].unsqueeze(2).to_broadcast([P, CHUNK_NODES, ANCHORS]),
+                    table_sb[:, nodes].unsqueeze(2).to_broadcast(shape),
                     start=False,
                     stop=True,
                 )
             else:
-                summed[c, k] = held.tile([P, CHUNK_NODES, ANCHORS], F32, name=f"summed{c}_{k}")
+                summed[c, k] = held.tile([P, size], F32, name=f"summed{c}_{k}")
                 nc.gpsimd.tensor_tensor(
-                    summed[c, k][:],
-                    scaled[c, k][:],
-                    own_sb[k][:, nodes].unsqueeze(2).to_broadcast([P, CHUNK_NODES, ANCHORS]),
+                    by_node(summed[c, k][:]),
+                    by_node(scaled[c, k][:]),
+                    own_sb[k][:, nodes].unsqueeze(2).to_broadcast(shape),
                     ADD,
                 )
 
@@ -147,11 +152,15 @@ def tile_p_a_gin_kernel(tc, table, w_nb, w_self, b, dist, score, offs, out):
         nc.scalar.mul(b_mean[:], b_sb[:], 1.0 / ANCHORS)
         mean = [held.tile([P, NODES], F32, name=f"mean{k}") for k in range(BLOCKS)]
         for c, k in banks:
-            nodes = slice(c * CHUNK_NODES, (c + 1) * CHUNK_NODES)
-            hidden = held.tile([P, CHUNK_NODES, ANCHORS], F32, name=f"hidden{c}_{k}")
+            start, size = CHUNKS[c]
+            nodes = slice(start // ANCHORS, (start + size) // ANCHORS)
+            hidden = held.tile([P, size], F32, name=f"hidden{c}_{k}")
             nc.scalar.activation(hidden[:], summed[c, k][:], RELU, bias=b_mean[:, k : k + 1], scale=1.0 / ANCHORS)
-            nc.vector.tensor_reduce(mean[k][:, nodes], hidden[:], axis=mybir.AxisListType.X, op=ADD)
+            nc.vector.tensor_reduce(mean[k][:, nodes], by_node(hidden[:]), axis=mybir.AxisListType.X, op=ADD)
 
+        early = CHUNKS[TENSOR_CHUNK][0] // ANCHORS
+        for k in range(BLOCKS):
+            nc.sync.dma_start(out[k * P : (k + 1) * P, :early], mean[k][:, :early])
         for k in range(BLOCKS):
             queue = nc.sync if k == 0 else nc.scalar
-            queue.dma_start(out[k * P : (k + 1) * P, :], mean[k][:])
+            queue.dma_start(out[k * P : (k + 1) * P, early:], mean[k][:, early:])

@@ -98,16 +98,7 @@ def tile_p_a_gin_kernel(tc, table, w_nb, w_self, b, dist, score, offs, out):
             d[c] = held.tile([P, size], F32, name=f"d{c}")
             nc.scalar.copy(d[c][:], d_ps[:])
 
-        banks = [(c, k) for c in range(len(CHUNKS)) for k in range(BLOCKS)]
-        scaled = {}
-        for c, k in banks:
-            if (c, k) == (0, 0):
-                spread_d(0)
-                for block in range(BLOCKS):
-                    nc.scalar.copy(own_sb[block][:], own_ps[:, block, :])
-            elif (c, k) == (1, 0):
-                for later in range(1, len(CHUNKS)):
-                    spread_d(later)
+        def look_up(c, k):
             start, size = CHUNKS[c]
             bank = psum.tile([P, size], F32, name="bank", tag="bank")
             for i in range(size // PIECE):
@@ -119,8 +110,21 @@ def tile_p_a_gin_kernel(tc, table, w_nb, w_self, b, dist, score, offs, out):
                     start=True,
                     stop=True,
                 )
-            scaled[c, k] = held.tile([P, size], F32, name=f"scaled{c}_{k}")
-            nc.vector.tensor_tensor(scaled[c, k][:], bank[:], d[c][:], MULT)
+            return bank
+
+        banks = [(c, k) for c in range(len(CHUNKS)) for k in range(BLOCKS)]
+        scaled = {}
+        for c in range(len(CHUNKS)):
+            looked_up = [look_up(c, k) for k in range(BLOCKS)]
+            if c == 0:
+                spread_d(0)
+                for k in range(BLOCKS):
+                    nc.scalar.copy(own_sb[k][:], own_ps[:, k, :])
+                for later in range(1, len(CHUNKS)):
+                    spread_d(later)
+            for k in range(BLOCKS):
+                scaled[c, k] = held.tile([P, CHUNKS[c][1]], F32, name=f"scaled{c}_{k}")
+                nc.vector.tensor_tensor(scaled[c, k][:], looked_up[k][:], d[c][:], MULT)
 
         identity = held.tile([P, P], F32, name="identity")
         make_identity(nc, identity[:])

import concourse.mybir as mybir
from concourse.masks import make_identity

BF16, F32, U16 = mybir.dt.bfloat16, mybir.dt.float32, mybir.dt.uint16
MULT, ADD, SUB = mybir.AluOpType.mult, mybir.AluOpType.add, mybir.AluOpType.subtract
RELU = mybir.ActivationFunctionType.Relu

P = 128
NODES = 256
ANCHORS = 8
ENTRIES = NODES * ANCHORS
BLOCKS = 2
PIECE = NODES
PIECE_COLS = PIECE // 16
BANK = 512
HALF = BANK // 2
CHUNKS = [(0, HALF)] + [(start, BANK) for start in range(HALF, ENTRIES - HALF, BANK)] + [(ENTRIES - HALF, HALF)]
LOOKUP_BANKS = 3
D_BANKS = 4
TENSOR_CHUNK = len(CHUNKS) - 2
ROW = 64
ROWS = ENTRIES // ROW
PARTS = 3

FLOPS = 2 * P * (BLOCKS * P) * (ENTRIES + NODES)


def leading_part(ap):
    return ap.bitcast(BF16).rearrange("p (n two) -> p n two", two=2)[:, :, 1]


def tile_p_a_gin_kernel(tc, table, w_nb, w_self, b, dist, score, offs, out):
    nc = tc.nc
    with (
        tc.tile_pool(name="held", bufs=1) as held,
        tc.psum_pool(name="psum_own", bufs=1) as psum_own,
        tc.psum_pool(name="psum_d", bufs=D_BANKS) as psum_d,
        tc.psum_pool(name="psum", bufs=LOOKUP_BANKS) as psum,
    ):
        dist_rows = held.tile([PARTS * ROWS, ROW], F32, name="dist_rows")
        for g in range(PARTS):
            nc.sync.dma_start(dist_rows[g * ROWS : (g + 1) * ROWS, :], dist.rearrange("o (q n) -> (o q) n", q=ROWS))
        score_sb = held.tile([P, ANCHORS], F32, name="score_sb")
        nc.scalar.dma_start(score_sb[:], score.broadcast_to([P, ANCHORS]))
        table_sb = held.tile([P, NODES], BF16, name="table_sb")
        nc.sync.dma_start(table_sb[:], table)
        w_self_sb = held.tile([P, BLOCKS * P], BF16, name="w_self_sb")
        nc.scalar.dma_start(w_self_sb[:], w_self)
        offsets = held.tile([P, ENTRIES // 16], U16, name="offsets")
        nc.sync.dma_start(offsets[:], offs)
        w_nb_sb = held.tile([P, BLOCKS * P], BF16, name="w_nb_sb")
        nc.scalar.dma_start(w_nb_sb[:], w_nb)
        b_sb = held.tile([P, BLOCKS], F32, name="b_sb")
        nc.gpsimd.dma_start(b_sb[:], b.rearrange("(k p) o -> p (k o)", p=P))

        ones = held.tile([P, ROWS], F32, name="ones")
        nc.vector.memset(ones[:], 1.0)
        count_columns = held.tile([P, ROWS], F32, name="count_columns", align_bytes=64)
        nc.vector.tensor_tensor_scan(count_columns[:], ones[:], ones[:], 0.0, MULT, ADD)
        count_rows = held.tile([P, ROWS], F32, name="count_rows", align_bytes=64)
        nc.vector.transpose(count_rows[:], count_columns[:])
        pick = held.tile([P, ROWS], BF16, name="pick")
        nc.vector.tensor_tensor(pick[:], count_rows[:], count_columns[:], mybir.AluOpType.is_equal)

        parts = held.tile([P, ROW], F32, name="parts")
        nc.vector.memset(parts[PARTS * ROWS :, :], 0.0)
        nc.vector.tensor_tensor(
            parts[: PARTS * ROWS, :].rearrange("p (n a) -> p n a", a=ANCHORS),
            dist_rows[:].rearrange("p (n a) -> p n a", a=ANCHORS),
            score_sb[: PARTS * ROWS, :].unsqueeze(1).to_broadcast([PARTS * ROWS, ROW // ANCHORS, ANCHORS]),
            MULT,
        )
        for rows in (2 * ROWS, ROWS):
            nc.vector.tensor_tensor(parts[:rows, :], parts[:rows, :], leading_part(parts[:rows, :]), SUB)

        own_ps = psum_own.tile([P, BLOCKS, NODES], F32, name="own_ps")
        own_sb = [held.tile([P, NODES], F32, name=f"own_sb{k}") for k in range(BLOCKS)]
        for k in range(BLOCKS):
            nc.tensor.matmul(own_ps[:, k, :], w_self_sb[:, k * P : (k + 1) * P], table_sb[:], start=True, stop=True)

        d = {}

        def by_node(ap):
            return ap.rearrange("p (n a) -> p n a", a=ANCHORS)

        def spread_d(c):
            start, size = CHUNKS[c]
            d_ps = psum_d.tile([P, size], F32, name=f"d_ps{c}", tag="d_ps")
            for i in range(size // ROW):
                q = start // ROW + i
                nc.tensor.matmul(
                    d_ps[:, i * ROW : (i + 1) * ROW],
                    pick[:, q : q + 1].to_broadcast([P, P]),
                    leading_part(parts[:]),
                    start=True,
                    stop=True,
                )
            d[c] = held.tile([P, size], F32, name=f"d{c}")
            nc.scalar.copy(d[c][:], d_ps[:])

        def look_up(c, k):
            start, size = CHUNKS[c]
            bank = psum.tile([P, size], F32, name="bank", tag="bank")
            for i in range(size // PIECE):
                piece = start // PIECE + i
                nc.tensor.matmul(
                    bank[:, i * PIECE : (i + 1) * PIECE],
                    w_nb_sb[:, k * P : (k + 1) * P],
                    table_sb[:].indirect(offsets[:, piece * PIECE_COLS : (piece + 1) * PIECE_COLS]),
                    start=True,
                    stop=True,
                )
            return bank

        banks = [(c, k) for c in range(len(CHUNKS)) for k in range(BLOCKS)]
        scaled = {}
        for c in range(len(CHUNKS)):
            looked_up = [look_up(c, k) for k in range(BLOCKS)]
            if c == 0:
                spread_d(0)
                for k in range(BLOCKS):
                    nc.scalar.copy(own_sb[k][:], own_ps[:, k, :])
                for later in range(1, len(CHUNKS)):
                    spread_d(later)
            for k in range(BLOCKS):
                scaled[c, k] = held.tile([P, CHUNKS[c][1]], F32, name=f"scaled{c}_{k}")
                nc.vector.tensor_tensor(scaled[c, k][:], looked_up[k][:], d[c][:], MULT)

        identity = held.tile([P, P], F32, name="identity")
        make_identity(nc, identity[:])
        summed = {}
        for c, k in banks:
            start, size = CHUNKS[c]
            nodes = slice(start // ANCHORS, (start + size) // ANCHORS)
            shape = [P, size // ANCHORS, ANCHORS]
            if c == TENSOR_CHUNK:
                summed[c, k] = psum_d.tile([P, size], F32, name=f"summed{c}_{k}", tag="d_ps")
                nc.tensor.matmul(summed[c, k][:], identity[:], scaled[c, k][:], start=True, stop=False)
                nc.tensor.matmul(
                    by_node(summed[c, k][:]),
                    w_self_sb[:, k * P : (k + 1) * P],
                    table_sb[:, nodes].unsqueeze(2).to_broadcast(shape),
                    start=False,
                    stop=True,
                )
            else:
                summed[c, k] = held.tile([P, size], F32, name=f"summed{c}_{k}")
                nc.gpsimd.tensor_tensor(
                    by_node(summed[c, k][:]),
                    by_node(scaled[c, k][:]),
                    own_sb[k][:, nodes].unsqueeze(2).to_broadcast(shape),
                    ADD,
                )

        b_mean = held.tile([P, BLOCKS], F32, name="b_mean")
        nc.scalar.mul(b_mean[:], b_sb[:], 1.0 / ANCHORS)
        mean = [held.tile([P, NODES], F32, name=f"mean{k}") for k in range(BLOCKS)]
        for c, k in banks:
            start, size = CHUNKS[c]
            nodes = slice(start // ANCHORS, (start + size) // ANCHORS)
            hidden = held.tile([P, size], F32, name=f"hidden{c}_{k}")
            nc.scalar.activation(hidden[:], summed[c, k][:], RELU, bias=b_mean[:, k : k + 1], scale=1.0 / ANCHORS)
            nc.vector.tensor_reduce(mean[k][:, nodes], by_node(hidden[:]), axis=mybir.AxisListType.X, op=ADD)

        early = CHUNKS[TENSOR_CHUNK][0] // ANCHORS
        for k in range(BLOCKS):
            nc.sync.dma_start(out[k * P : (k + 1) * P, :early], mean[k][:, :early])
        for k in range(BLOCKS):
            queue = nc.sync if k == 0 else nc.scalar
            queue.dma_start(out[k * P : (k + 1) * P, early:], mean[k][:, early:])
